import numpy as np
import ml_dtypes


def mxq(x, axis, fmt="e4m3"):
    dtype, down = {"e4m3": (ml_dtypes.float8_e4m3fn, 7), "e5m2": (ml_dtypes.float8_e5m2, 14)}[fmt]
    v = np.moveaxis(np.asarray(x, np.float32).astype(ml_dtypes.bfloat16).astype(np.float64), axis, -1)
    blocks = v.reshape(v.shape[:-1] + (-1, 32))
    amax = np.abs(blocks).max(-1, keepdims=True)
    byte = np.maximum(np.where(amax > 0, np.frexp(amax)[1] - 1 + 127, 0) - down, 1)
    scale = np.exp2(byte - 127.0)
    codes = (blocks / scale).astype(np.float32).astype(dtype).astype(np.float64)
    return np.moveaxis((codes * scale).reshape(v.shape), -1, axis)


WIDE = False


def mx_kscale(k):
    if not WIDE:
        return np.ones(k)
    levels = np.array([10, -10, 5, -5, 0])
    if k % 512:
        return np.exp2(np.random.permutation(np.resize(levels, k // 32))).repeat(32)
    a = np.empty((k // 512, 16))
    for p in range(k // 512):
        a[p, :8] = np.random.permutation(np.resize(levels, 8))
        for g in range(8):
            far = levels[np.abs(levels - a[p, g]) >= 10]
            a[p, g + 8] = far[np.random.randint(len(far))]
    return np.exp2(a.ravel()).repeat(32)


BF16 = ml_dtypes.bfloat16


def bf(x):
    return np.asarray(x, np.float32).astype(BF16)


def f64(x):
    return np.asarray(x).astype(np.float64)


N, D, H, E = 256, 512, 8192, 2

CLAMP_MAX = float(np.log(100.0))


def setup_inputs():
    s, t = mx_kscale(D), mx_kscale(H)
    return {"x": bf(np.random.standard_normal((N, D)) * s),
            "W1": bf(np.random.standard_normal((E, D, H)) / np.sqrt(D) / s[:, None] * t),
            "b1": bf(np.random.standard_normal((E, H)) * 0.1 * t),
            "W2": bf(np.random.standard_normal((E, H, D)) / np.sqrt(H) / t[:, None]),
            "b2": bf(np.random.standard_normal((E, D)) * 0.1),
            "temperature": bf(np.log(2.0) + 0.1 * np.random.standard_normal((1,)))}


def reference(x, W1, b1, W2, b2, temperature):
    xe = f64(x).reshape(E, N // E, D)
    h = np.maximum((mxq(xe, 2, "e4m3") @ mxq(f64(W1), 1, "e4m3")) + f64(b1)[:, None, :], 0.0)
    y = (mxq(h, 2, "e4m3") @ mxq(f64(W2), 1, "e4m3")) + f64(b2)[:, None, :]
    logit_scale = np.exp(np.minimum(f64(temperature), CLAMP_MAX))
    return y.reshape(N, D) * logit_scale

@@ -1,0 +1,274 @@
+import math
+from contextlib import ExitStack
+
+import concourse.mybir as mybir
+from concourse.masks import make_identity
+
+BF16 = mybir.dt.bfloat16
+F32 = mybir.dt.float32
+U32 = mybir.dt.uint32
+U8 = mybir.dt.uint8
+FP8X4 = mybir.dt.float8_e4m3fn_x4
+ALU = mybir.AluOpType
+ACT = mybir.ActivationFunctionType
+
+P = 128
+PACK = 4
+K_PASS = P * PACK
+
+E = 2
+TOKENS = 128
+D = 512
+H = 8192
+PASSES = H // K_PASS
+
+UNIT = 1024
+UNIT_PASSES = UNIT // D
+EXPERT_UNITS = H // UNIT
+N_UNITS = E * EXPERT_UNITS
+LEAD = 3
+LOAD_AHEAD = 7
+
+VECTOR_WORDS = 336
+
+B2_LOAD_STEP = N_UNITS // 2
+B2_SCALE_STEP = B2_LOAD_STEP + 4
+
+CLAMP_MAX = math.log(100.0)
+
+FLOPS = 2 * (2 * E * TOKENS * D * H)
+
+
+def tile_moelayer_k_kernel(tc, x, W1, b1, W2, b2, temperature, out):
+    nc = tc.nc
+    with ExitStack() as stack:
+        stack.enter_context(nc.allow_non_contiguous_dma(reason="temperature: one element a partition"))
+        stack.enter_context(tc.manual_schedule())
+        const = stack.enter_context(tc.tile_pool(name="const", bufs=1))
+        raw_pool = stack.enter_context(tc.tile_pool(name="raw", bufs=LOAD_AHEAD + 1))
+        grouped_pool = stack.enter_context(tc.tile_pool(name="grouped", bufs=4))
+        operand_pool = stack.enter_context(tc.tile_pool(name="operand", bufs=3))
+        hidden_pool = stack.enter_context(tc.tile_pool(name="hidden", bufs=LEAD + 1))
+        psum_setup = stack.enter_context(tc.psum_pool(name="psum_setup", bufs=1))
+        psum_hidden = stack.enter_context(tc.psum_pool(name="psum_hidden", bufs=2 * UNIT_PASSES))
+        psum_y = stack.enter_context(tc.psum_pool(name="psum_y", bufs=E))
+
+        def load_unit(weight, j):
+            e, i = j // EXPERT_UNITS, j % EXPERT_UNITS
+            raw = raw_pool.tile([P, PACK, UNIT], BF16, name="raw")
+            if weight == "W1":
+                columns = W1[e, :, i * UNIT : (i + 1) * UNIT]
+                nc.sync.dma_start(out=raw[:], in_=columns.rearrange("(p t) w -> p t w", t=PACK))
+            else:
+                for q in range(UNIT_PASSES):
+                    g = i * UNIT_PASSES + q
+                    rows = W2[e, g * K_PASS : (g + 1) * K_PASS, :]
+                    nc.sync.dma_start(
+                        out=raw[:, :, q * D : (q + 1) * D],
+                        in_=rows.rearrange("(p t) d -> p t d", t=PACK),
+                    )
+            return raw
+
+        def regroup(weight, raw):
+            grouped = grouped_pool.tile([P, UNIT, PACK], BF16, name="grouped", align_bytes=64)
+
+            def views(first, last):
+                if weight == "W1":
+                    m = slice(first // (UNIT_PASSES * PACK), last // (UNIT_PASSES * PACK))
+                    to = grouped[:].rearrange("p (q u m) t -> p q m t u", q=UNIT_PASSES, u=PACK)
+                    frm = raw[:].rearrange("p t (q m u) -> p q m t u", q=UNIT_PASSES, u=PACK)
+                    return to[:, :, m, :, :], frm[:, :, m, :, :]
+                return (
+                    grouped[:, first:last, :].rearrange("p (c i) t -> p c t i", i=4),
+                    raw[:, :, first:last].rearrange("p t (c i) -> p c t i", i=4),
+                )
+
+            to, frm = views(0, VECTOR_WORDS)
+            nc.vector.tensor_copy(out=to, in_=frm)
+            to, frm = views(VECTOR_WORDS, UNIT)
+            nc.scalar.copy(out=to, in_=frm)
+            return grouped
+
+        def quantise(grouped):
+            words = operand_pool.tile([P, UNIT], U32, name="words", align_bytes=64)
+            scales = operand_pool.tile([P, UNIT], U8, name="scales", align_bytes=64)
+            nc.vector.quantize_mx(
+                out=words[:].bitcast(FP8X4),
+                scales=scales[:],
+                in_=grouped[:].rearrange("p w t -> p (w t)"),
+            )
+            return words, scales
+
+        stream = [("W1", j) for j in range(LEAD)]
+        for j in range(N_UNITS - LEAD):
+            stream.extend([("W2", j), ("W1", j + LEAD)])
+        stream.extend([("W2", j) for j in range(N_UNITS - LEAD, N_UNITS)])
+
+        def unit_at(s):
+            return stream[s] if 0 <= s < len(stream) else (None, None)
+
+        temp = const.tile([P, 1], BF16)
+        nc.scalar.dma_start(out=temp[:], in_=temperature.partition_broadcast(P))
+        x_rows = const.tile([P, E, D], BF16)
+        nc.scalar.dma_start(out=x_rows[:], in_=x.rearrange("(e n) k -> n e k", e=E))
+        b1_rows = const.tile([P, K_PASS], BF16)
+        nc.vector.memset(b1_rows[:], 0.0)
+        nc.scalar.dma_start(
+            out=b1_rows[0 : E * PASSES, :], in_=b1.rearrange("e (g c) -> (e g) c", c=K_PASS)
+        )
+
+        raws = {}
+        for s in range(LOAD_AHEAD):
+            raws[s] = load_unit(*stream[s])
+
+        identity = const.tile([P, P], BF16)
+        make_identity(nc, identity[:])
+
+        temp_clamped = const.tile([P, 1], F32)
+        nc.vector.tensor_scalar_min(out=temp_clamped[:], in0=temp[:], scalar1=CLAMP_MAX)
+        logit_scale = const.tile([P, 1], F32)
+        nc.scalar.activation(out=logit_scale[:], in_=temp_clamped[:], func=ACT.Exp)
+
+        x_words = const.tile([P, E * TOKENS], U32, align_bytes=64)
+        x_scales = const.tile([P, E * TOKENS], U8, align_bytes=64)
+        b1_t = const.tile([P, E * PASSES, PACK], F32)
+
+        def prepare_x_and_b1():
+            x_t = psum_setup.tile([P, E, PACK, TOKENS], BF16)
+            for e in range(E):
+                for t in range(PACK):
+                    nc.tensor.transpose(
+                        x_t[:, e, t, :], x_rows[:, e, t : K_PASS : PACK], identity[:]
+                    )
+            x_grouped = const.tile([P, E, TOKENS, PACK], BF16, align_bytes=64)
+            nc.vector.tensor_copy(out=x_grouped[:], in_=x_t[:].rearrange("p e t n -> p e n t"))
+            b1_t_psum = psum_setup.tile([P, PACK, P], BF16)
+            for t in range(PACK):
+                nc.tensor.transpose(
+                    b1_t_psum[:, t, :], b1_rows[:, t : K_PASS : PACK], identity[:]
+                )
+            nc.vector.tensor_copy(
+                out=b1_t[:], in_=b1_t_psum[:, :, 0 : E * PASSES].rearrange("p t r -> p r t")
+            )
+            nc.vector.quantize_mx(
+                out=x_words[:].bitcast(FP8X4),
+                scales=x_scales[:],
+                in_=x_grouped[:].rearrange("p e n t -> p (e n t)"),
+            )
+
+        b2_all = const.tile([P, E * D], BF16)
+        b2_scaled = const.tile([P, E * D], F32)
+
+        def first_matmul(j, w1_words, w1_scales):
+            tokens = slice((j // EXPERT_UNITS) * TOKENS, (j // EXPERT_UNITS + 1) * TOKENS)
+            product = []
+            for q in range(UNIT_PASSES):
+                bank = psum_hidden.tile([P, PACK, TOKENS], F32, name="bank")
+                for t in range(PACK):
+                    columns = slice((q * PACK + t) * P, (q * PACK + t + 1) * P)
+                    nc.tensor.matmul_mx(
+                        out=bank[:, t, :],
+                        lhsT=w1_words[:, columns].bitcast(FP8X4),
+                        lhsT_scale=w1_scales[:, columns],
+                        rhs=x_words[:, tokens].bitcast(FP8X4),
+                        rhs_scale=x_scales[:, tokens],
+                        start=True,
+                        stop=True,
+                    )
+                product.append(bank)
+            return product
+
+        def add_bias(j, product):
+            biased = hidden_pool.tile([P, UNIT_PASSES, TOKENS, PACK], BF16, name="biased")
+            for q in range(UNIT_PASSES):
+                nc.vector.tensor_tensor(
+                    out=biased[:, q, :, :],
+                    in0=product[q][:].rearrange("p t n -> p n t"),
+                    in1=b1_t[:, j * UNIT_PASSES + q : j * UNIT_PASSES + q + 1, :].to_broadcast([P, TOKENS, PACK]),
+                    op=ALU.add,
+                )
+            return biased
+
+        def relu(biased):
+            h = hidden_pool.tile([P, UNIT_PASSES * TOKENS * PACK], BF16, name="h", align_bytes=64)
+            nc.vector.tensor_scalar_max(
+                out=h[:], in0=biased[:].rearrange("p q n t -> p (q n t)"), scalar1=0.0
+            )
+            return h
+
+        def quantise_hidden(h):
+            h_words = hidden_pool.tile([P, UNIT_PASSES * TOKENS], U32, name="h_words", align_bytes=64)
+            h_scales = hidden_pool.tile([P, UNIT_PASSES * TOKENS], U8, name="h_scales", align_bytes=64)
+            nc.vector.quantize_mx(out=h_words[:].bitcast(FP8X4), scales=h_scales[:], in_=h[:])
+            return h_words, h_scales
+
+        def second_matmul(j, y, h_words, h_scales, w2_words, w2_scales):
+            for q in range(UNIT_PASSES):
+                g = (j % EXPERT_UNITS) * UNIT_PASSES + q
+                nc.tensor.matmul_mx(
+                    out=y[:],
+                    lhsT=h_words[:, q * TOKENS : (q + 1) * TOKENS].bitcast(FP8X4),
+                    lhsT_scale=h_scales[:, q * TOKENS : (q + 1) * TOKENS],
+                    rhs=w2_words[:, q * D : (q + 1) * D].bitcast(FP8X4),
+                    rhs_scale=w2_scales[:, q * D : (q + 1) * D],
+                    start=(g == 0),
+                    stop=(g == PASSES - 1),
+                )
+
+        def finish(e, y):
+            result = hidden_pool.tile([P, D], F32, name="result")
+            nc.vector.scalar_tensor_tensor(
+                out=result[:],
+                in0=y[:],
+                scalar=logit_scale[:, 0:1],
+                in1=b2_scaled[:, e * D : (e + 1) * D],
+                op0=ALU.mult,
+                op1=ALU.add,
+            )
+            nc.sync.dma_start(out=out[e * TOKENS : (e + 1) * TOKENS, :], in_=result[:])
+
+        groupeds = {}
+        products = {}
+        biaseds = {}
+        hs = {}
+        h_operands = {}
+        ys = {}
+        for s in range(len(stream) + 2):
+            if s + LOAD_AHEAD < len(stream):
+                raws[s + LOAD_AHEAD] = load_unit(*stream[s + LOAD_AHEAD])
+            if s < len(stream):
+                groupeds[s] = regroup(stream[s][0], raws[s])
+            if s == 0:
+                prepare_x_and_b1()
+            if s == B2_LOAD_STEP:
+                nc.sync.dma_start(
+                    out=b2_all[:], in_=b2.rearrange("e d -> (e d)").partition_broadcast(P)
+                )
+            if s == B2_SCALE_STEP:
+                nc.vector.tensor_scalar_mul(
+                    out=b2_scaled[:], in0=b2_all[:], scalar1=logit_scale[:, 0:1]
+                )
+
+            weight, j = unit_at(s - 4)
+            if weight == "W1":
+                h_operands[j] = quantise_hidden(hs[j])
+
+            weight, j = unit_at(s - 3)
+            if weight == "W1":
+                biaseds[j] = add_bias(j, products[j])
+
+            weight, j = unit_at(s - 1)
+            if weight == "W1":
+                products[j] = first_matmul(j, *quantise(groupeds[s - 1]))
+            if weight == "W2":
+                if j % EXPERT_UNITS == 0:
+                    ys[j // EXPERT_UNITS] = psum_y.tile([P, D], F32, name="y")
+                second_matmul(j, ys[j // EXPERT_UNITS], *h_operands[j], *quantise(groupeds[s - 1]))
+
+            weight, j = unit_at(s - 3)
+            if weight == "W1":
+                hs[j] = relu(biaseds[j])
+
+            weight, j = unit_at(s - 2)
+            if weight == "W2" and j % EXPERT_UNITS == EXPERT_UNITS - 1:
+                finish(j // EXPERT_UNITS, ys[j // EXPERT_UNITS])

@@ -29,7 +29,10 @@ N_UNITS = E * EXPERT_UNITS
 LEAD = 3
 LOAD_AHEAD = 7
 
-VECTOR_WORDS = 336
+VECTOR_COLUMNS = 168
+HEAD_PIECE = 256
+HEAD_UNITS = 2
+HEAD_VECTOR_COLUMNS = 160
 
 B2_LOAD_STEP = N_UNITS // 2
 B2_SCALE_STEP = B2_LOAD_STEP + 4
@@ -53,12 +56,16 @@ def tile_moelayer_k_kernel(tc, x, W1, b1, W2, b2, temperature, out):
         psum_hidden = stack.enter_context(tc.psum_pool(name="psum_hidden", bufs=2 * UNIT_PASSES))
         psum_y = stack.enter_context(tc.psum_pool(name="psum_y", bufs=E))
 
-        def load_unit(weight, j):
+        def load_unit(weight, j, piece=UNIT):
             e, i = j // EXPERT_UNITS, j % EXPERT_UNITS
             raw = raw_pool.tile([P, PACK, UNIT], BF16, name="raw")
             if weight == "W1":
-                columns = W1[e, :, i * UNIT : (i + 1) * UNIT]
-                nc.sync.dma_start(out=raw[:], in_=columns.rearrange("(p t) w -> p t w", t=PACK))
+                for first in range(0, UNIT, piece):
+                    columns = W1[e, :, i * UNIT + first : i * UNIT + first + piece]
+                    nc.sync.dma_start(
+                        out=raw[:, :, first : first + piece],
+                        in_=columns.rearrange("(p t) w -> p t w", t=PACK),
+                    )
             else:
                 for q in range(UNIT_PASSES):
                     g = i * UNIT_PASSES + q
@@ -69,24 +76,31 @@ def tile_moelayer_k_kernel(tc, x, W1, b1, W2, b2, temperature, out):
                     )
             return raw
 
+        def views(weight, grouped, raw, q, first, last):
+            order = "p (q u m) t -> p q m t u" if weight == "W1" else "p (q m u) t -> p q m t u"
+            fours = slice(first // PACK, last // PACK)
+            to = grouped[:].rearrange(order, q=UNIT_PASSES, u=PACK)
+            frm = raw[:].rearrange("p t (q m u) -> p q m t u", q=UNIT_PASSES, u=PACK)
+            return to[:, q, fours, :, :], frm[:, q, fours, :, :]
+
         def regroup(weight, raw):
             grouped = grouped_pool.tile([P, UNIT, PACK], BF16, name="grouped", align_bytes=64)
-
-            def views(first, last):
-                if weight == "W1":
-                    m = slice(first // (UNIT_PASSES * PACK), last // (UNIT_PASSES * PACK))
-                    to = grouped[:].rearrange("p (q u m) t -> p q m t u", q=UNIT_PASSES, u=PACK)
-                    frm = raw[:].rearrange("p t (q m u) -> p q m t u", q=UNIT_PASSES, u=PACK)
-                    return to[:, :, m, :, :], frm[:, :, m, :, :]
-                return (
-                    grouped[:, first:last, :].rearrange("p (c i) t -> p c t i", i=4),
-                    raw[:, :, first:last].rearrange("p t (c i) -> p c t i", i=4),
-                )
-
-            to, frm = views(0, VECTOR_WORDS)
+            both = slice(0, UNIT_PASSES)
+            to, frm = views(weight, grouped, raw, both, 0, VECTOR_COLUMNS)
             nc.vector.tensor_copy(out=to, in_=frm)
-            to, frm = views(VECTOR_WORDS, UNIT)
+            to, frm = views(weight, grouped, raw, both, VECTOR_COLUMNS, D)
             nc.scalar.copy(out=to, in_=frm)
+            return grouped
+
+        def regroup_in_pieces(weight, raw, vector_columns):
+            grouped = grouped_pool.tile([P, UNIT, PACK], BF16, name="grouped", align_bytes=64)
+            for q in range(UNIT_PASSES):
+                for first in range(0, D, HEAD_PIECE):
+                    middle = first + vector_columns
+                    to, frm = views(weight, grouped, raw, q, first, middle)
+                    nc.vector.tensor_copy(out=to, in_=frm)
+                    to, frm = views(weight, grouped, raw, q, middle, first + HEAD_PIECE)
+                    nc.scalar.copy(out=to, in_=frm)
             return grouped
 
         def quantise(grouped):
@@ -107,27 +121,33 @@ def tile_moelayer_k_kernel(tc, x, W1, b1, W2, b2, temperature, out):
         def unit_at(s):
             return stream[s] if 0 <= s < len(stream) else (None, None)
 
-        temp = const.tile([P, 1], BF16)
-        nc.scalar.dma_start(out=temp[:], in_=temperature.partition_broadcast(P))
-        x_rows = const.tile([P, E, D], BF16)
-        nc.scalar.dma_start(out=x_rows[:], in_=x.rearrange("(e n) k -> n e k", e=E))
+        warm = const.tile([P, 1], F32)
+        nc.vector.memset(warm[:], 0.0)
+        nc.scalar.activation(out=warm[:], in_=warm[:], func=ACT.Exp)
+
         b1_rows = const.tile([P, K_PASS], BF16)
         nc.vector.memset(b1_rows[:], 0.0)
-        nc.scalar.dma_start(
-            out=b1_rows[0 : E * PASSES, :], in_=b1.rearrange("e (g c) -> (e g) c", c=K_PASS)
-        )
-
-        raws = {}
-        for s in range(LOAD_AHEAD):
-            raws[s] = load_unit(*stream[s])
-
         identity = const.tile([P, P], BF16)
         make_identity(nc, identity[:])
 
+        raws = {}
+        raws[0] = load_unit(*stream[0], piece=HEAD_PIECE)
+        x_rows = const.tile([P, E, D], BF16)
+        nc.sync.dma_start(out=x_rows[:], in_=x.rearrange("(e n) k -> n e k", e=E))
+        nc.scalar.dma_start(
+            out=b1_rows[0 : E * PASSES, :], in_=b1.rearrange("e (g c) -> (e g) c", c=K_PASS)
+        )
+        temp = const.tile([P, 1], BF16)
+        nc.scalar.dma_start(out=temp[:], in_=temperature.partition_broadcast(P))
+        for s in range(1, LOAD_AHEAD):
+            raws[s] = load_unit(*stream[s], piece=HEAD_PIECE if s < HEAD_UNITS else UNIT)
+
         temp_clamped = const.tile([P, 1], F32)
-        nc.vector.tensor_scalar_min(out=temp_clamped[:], in0=temp[:], scalar1=CLAMP_MAX)
         logit_scale = const.tile([P, 1], F32)
-        nc.scalar.activation(out=logit_scale[:], in_=temp_clamped[:], func=ACT.Exp)
+
+        def prepare_scale():
+            nc.vector.tensor_scalar_min(out=temp_clamped[:], in0=temp[:], scalar1=CLAMP_MAX)
+            nc.scalar.activation(out=logit_scale[:], in_=temp_clamped[:], func=ACT.Exp)
 
         x_words = const.tile([P, E * TOKENS], U32, align_bytes=64)
         x_scales = const.tile([P, E * TOKENS], U8, align_bytes=64)
@@ -237,9 +257,16 @@ def tile_moelayer_k_kernel(tc, x, W1, b1, W2, b2, temperature, out):
             if s + LOAD_AHEAD < len(stream):
                 raws[s + LOAD_AHEAD] = load_unit(*stream[s + LOAD_AHEAD])
             if s < len(stream):
-                groupeds[s] = regroup(stream[s][0], raws[s])
+                if s == 0:
+                    groupeds[s] = regroup_in_pieces(stream[s][0], raws[s], HEAD_VECTOR_COLUMNS)
+                elif s < HEAD_UNITS:
+                    groupeds[s] = regroup_in_pieces(stream[s][0], raws[s], HEAD_PIECE // 2)
+                else:
+                    groupeds[s] = regroup(stream[s][0], raws[s])
             if s == 0:
                 prepare_x_and_b1()
+            if s == 4:
+                prepare_scale()
             if s == B2_LOAD_STEP:
                 nc.sync.dma_start(
                     out=b2_all[:], in_=b2.rearrange("e d -> (e d)").partition_broadcast(P)

@@ -26,10 +26,13 @@ UNIT = 1024
 UNIT_PASSES = UNIT // D
 EXPERT_UNITS = H // UNIT
 N_UNITS = E * EXPERT_UNITS
-LEAD = 3
+LEAD = 4
+PAIR = 2
 LOAD_AHEAD = 7
 
-VECTOR_COLUMNS = 168
+VECTOR_COLUMNS = {"W1": 172, "W2": 140}
+TENSOR_COLUMNS = 192
+STAGE_AHEAD = 2
 HEAD_PIECE = 256
 HEAD_UNITS = 2
 HEAD_VECTOR_COLUMNS = 160
@@ -52,7 +55,7 @@ def tile_moelayer_k_kernel(tc, x, W1, b1, W2, b2, temperature, out):
         grouped_pool = stack.enter_context(tc.tile_pool(name="grouped", bufs=4))
         operand_pool = stack.enter_context(tc.tile_pool(name="operand", bufs=3))
         hidden_pool = stack.enter_context(tc.tile_pool(name="hidden", bufs=LEAD + 1))
-        psum_setup = stack.enter_context(tc.psum_pool(name="psum_setup", bufs=1))
+        psum_staged = stack.enter_context(tc.psum_pool(name="psum_staged", bufs=2))
         psum_hidden = stack.enter_context(tc.psum_pool(name="psum_hidden", bufs=2 * UNIT_PASSES))
         psum_y = stack.enter_context(tc.psum_pool(name="psum_y", bufs=E))
 
@@ -83,14 +86,35 @@ def tile_moelayer_k_kernel(tc, x, W1, b1, W2, b2, temperature, out):
             frm = raw[:].rearrange("p t (q m u) -> p q m t u", q=UNIT_PASSES, u=PACK)
             return to[:, q, fours, :, :], frm[:, q, fours, :, :]
 
-        def regroup(weight, raw):
+        def regroup(weight, raw, staged):
             grouped = grouped_pool.tile([P, UNIT, PACK], BF16, name="grouped", align_bytes=64)
             both = slice(0, UNIT_PASSES)
-            to, frm = views(weight, grouped, raw, both, 0, VECTOR_COLUMNS)
+            middle = VECTOR_COLUMNS[weight]
+            to, frm = views(weight, grouped, raw, both, 0, middle)
             nc.vector.tensor_copy(out=to, in_=frm)
-            to, frm = views(weight, grouped, raw, both, VECTOR_COLUMNS, D)
-            nc.scalar.copy(out=to, in_=frm)
+            if weight == "W1":
+                to, frm = views(weight, grouped, raw, both, middle, D)
+                nc.scalar.copy(out=to, in_=frm)
+                return grouped
+            for q, last in ((0, D), (1, D - TENSOR_COLUMNS)):
+                to, frm = views(weight, grouped, raw, q, middle, last)
+                nc.scalar.copy(out=to, in_=frm)
+            nc.scalar.copy(out=grouped[:, UNIT - TENSOR_COLUMNS :, :], in_=staged[:])
             return grouped
+
+        def stage(raw):
+            first = UNIT - TENSOR_COLUMNS
+            staged = psum_staged.tile([P, TENSOR_COLUMNS, PACK], BF16, name="staged")
+            for w in range(0, TENSOR_COLUMNS, P):
+                last = min(w + P, TENSOR_COLUMNS)
+                nc.tensor.matmul(
+                    out=staged[:, w:last, :],
+                    lhsT=identity[:],
+                    rhs=raw[:, :, first + w : first + last].rearrange("p t w -> p w t"),
+                    start=True,
+                    stop=True,
+                )
+            return staged
 
         def regroup_in_pieces(weight, raw, vector_columns):
             grouped = grouped_pool.tile([P, UNIT, PACK], BF16, name="grouped", align_bytes=64)
@@ -103,14 +127,16 @@ def tile_moelayer_k_kernel(tc, x, W1, b1, W2, b2, temperature, out):
                     nc.scalar.copy(out=to, in_=frm)
             return grouped
 
-        def quantise(grouped):
+        def quantise(grouped, parts=1):
             words = operand_pool.tile([P, UNIT], U32, name="words", align_bytes=64)
             scales = operand_pool.tile([P, UNIT], U8, name="scales", align_bytes=64)
-            nc.vector.quantize_mx(
-                out=words[:].bitcast(FP8X4),
-                scales=scales[:],
-                in_=grouped[:].rearrange("p w t -> p (w t)"),
-            )
+            for part in range(parts):
+                span = slice(part * UNIT // parts, (part + 1) * UNIT // parts)
+                nc.vector.quantize_mx(
+                    out=words[:, span].bitcast(FP8X4),
+                    scales=scales[:, span],
+                    in_=grouped[:, span, :].rearrange("p w t -> p (w t)"),
+                )
             return words, scales
 
         stream = [("W1", j) for j in range(LEAD)]
@@ -154,7 +180,7 @@ def tile_moelayer_k_kernel(tc, x, W1, b1, W2, b2, temperature, out):
         b1_t = const.tile([P, E * PASSES, PACK], F32)
 
         def prepare_x_and_b1():
-            x_t = psum_setup.tile([P, E, PACK, TOKENS], BF16)
+            x_t = psum_staged.tile([P, E, PACK, TOKENS], BF16, name="staged")
             for e in range(E):
                 for t in range(PACK):
                     nc.tensor.transpose(
@@ -162,7 +188,7 @@ def tile_moelayer_k_kernel(tc, x, W1, b1, W2, b2, temperature, out):
                     )
             x_grouped = const.tile([P, E, TOKENS, PACK], BF16, align_bytes=64)
             nc.vector.tensor_copy(out=x_grouped[:], in_=x_t[:].rearrange("p e t n -> p e n t"))
-            b1_t_psum = psum_setup.tile([P, PACK, P], BF16)
+            b1_t_psum = psum_staged.tile([P, PACK, P], BF16, name="staged")
             for t in range(PACK):
                 nc.tensor.transpose(
                     b1_t_psum[:, t, :], b1_rows[:, t : K_PASS : PACK], identity[:]
@@ -198,37 +224,36 @@ def tile_moelayer_k_kernel(tc, x, W1, b1, W2, b2, temperature, out):
                 product.append(bank)
             return product
 
-        def add_bias(j, product):
-            biased = hidden_pool.tile([P, UNIT_PASSES, TOKENS, PACK], BF16, name="biased")
+        def add_bias(j, product, biased):
             for q in range(UNIT_PASSES):
                 nc.vector.tensor_tensor(
-                    out=biased[:, q, :, :],
+                    out=biased[:, j % PAIR, q, :, :],
                     in0=product[q][:].rearrange("p t n -> p n t"),
                     in1=b1_t[:, j * UNIT_PASSES + q : j * UNIT_PASSES + q + 1, :].to_broadcast([P, TOKENS, PACK]),
                     op=ALU.add,
                 )
-            return biased
 
         def relu(biased):
-            h = hidden_pool.tile([P, UNIT_PASSES * TOKENS * PACK], BF16, name="h", align_bytes=64)
+            h = hidden_pool.tile([P, PAIR * UNIT_PASSES * TOKENS * PACK], BF16, name="h", align_bytes=64)
             nc.vector.tensor_scalar_max(
-                out=h[:], in0=biased[:].rearrange("p q n t -> p (q n t)"), scalar1=0.0
+                out=h[:], in0=biased[:].rearrange("p j q n t -> p (j q n t)"), scalar1=0.0
             )
             return h
 
         def quantise_hidden(h):
-            h_words = hidden_pool.tile([P, UNIT_PASSES * TOKENS], U32, name="h_words", align_bytes=64)
-            h_scales = hidden_pool.tile([P, UNIT_PASSES * TOKENS], U8, name="h_scales", align_bytes=64)
+            h_words = hidden_pool.tile([P, PAIR * UNIT_PASSES * TOKENS], U32, name="h_words", align_bytes=64)
+            h_scales = hidden_pool.tile([P, PAIR * UNIT_PASSES * TOKENS], U8, name="h_scales", align_bytes=64)
             nc.vector.quantize_mx(out=h_words[:].bitcast(FP8X4), scales=h_scales[:], in_=h[:])
             return h_words, h_scales
 
         def second_matmul(j, y, h_words, h_scales, w2_words, w2_scales):
             for q in range(UNIT_PASSES):
                 g = (j % EXPERT_UNITS) * UNIT_PASSES + q
+                first = ((j % PAIR) * UNIT_PASSES + q) * TOKENS
                 nc.tensor.matmul_mx(
                     out=y[:],
-                    lhsT=h_words[:, q * TOKENS : (q + 1) * TOKENS].bitcast(FP8X4),
-                    lhsT_scale=h_scales[:, q * TOKENS : (q + 1) * TOKENS],
+                    lhsT=h_words[:, first : first + TOKENS].bitcast(FP8X4),
+                    lhsT_scale=h_scales[:, first : first + TOKENS],
                     rhs=w2_words[:, q * D : (q + 1) * D].bitcast(FP8X4),
                     rhs_scale=w2_scales[:, q * D : (q + 1) * D],
                     start=(g == 0),
@@ -237,16 +262,20 @@ def tile_moelayer_k_kernel(tc, x, W1, b1, W2, b2, temperature, out):
 
         def finish(e, y):
             result = hidden_pool.tile([P, D], F32, name="result")
-            nc.vector.scalar_tensor_tensor(
-                out=result[:],
-                in0=y[:],
-                scalar=logit_scale[:, 0:1],
-                in1=b2_scaled[:, e * D : (e + 1) * D],
-                op0=ALU.mult,
-                op1=ALU.add,
-            )
-            nc.sync.dma_start(out=out[e * TOKENS : (e + 1) * TOKENS, :], in_=result[:])
+            for half in (slice(0, D // 2), slice(D // 2, D)):
+                nc.vector.scalar_tensor_tensor(
+                    out=result[:, half],
+                    in0=y[:, half],
+                    scalar=logit_scale[:, 0:1],
+                    in1=b2_scaled[:, e * D + half.start : e * D + half.stop],
+                    op0=ALU.mult,
+                    op1=ALU.add,
+                )
+                nc.sync.dma_start(
+                    out=out[e * TOKENS : (e + 1) * TOKENS, half], in_=result[:, half]
+                )
 
+        stageds = {}
         groupeds = {}
         products = {}
         biaseds = {}
@@ -256,13 +285,16 @@ def tile_moelayer_k_kernel(tc, x, W1, b1, W2, b2, temperature, out):
         for s in range(len(stream) + 2):
             if s + LOAD_AHEAD < len(stream):
                 raws[s + LOAD_AHEAD] = load_unit(*stream[s + LOAD_AHEAD])
+            weight, j = unit_at(s + STAGE_AHEAD)
+            if weight == "W2":
+                stageds[s + STAGE_AHEAD] = stage(raws[s + STAGE_AHEAD])
             if s < len(stream):
                 if s == 0:
                     groupeds[s] = regroup_in_pieces(stream[s][0], raws[s], HEAD_VECTOR_COLUMNS)
                 elif s < HEAD_UNITS:
                     groupeds[s] = regroup_in_pieces(stream[s][0], raws[s], HEAD_PIECE // 2)
                 else:
-                    groupeds[s] = regroup(stream[s][0], raws[s])
+                    groupeds[s] = regroup(stream[s][0], raws[s], stageds.get(s))
             if s == 0:
                 prepare_x_and_b1()
             if s == 4:
@@ -277,12 +309,16 @@ def tile_moelayer_k_kernel(tc, x, W1, b1, W2, b2, temperature, out):
                 )
 
             weight, j = unit_at(s - 4)
-            if weight == "W1":
-                h_operands[j] = quantise_hidden(hs[j])
+            if weight == "W1" and j % PAIR == PAIR - 1:
+                h_operands[j // PAIR] = quantise_hidden(hs[j // PAIR])
 
             weight, j = unit_at(s - 3)
             if weight == "W1":
-                biaseds[j] = add_bias(j, products[j])
+                if j % PAIR == 0:
+                    biaseds[j // PAIR] = hidden_pool.tile(
+                        [P, PAIR, UNIT_PASSES, TOKENS, PACK], BF16, name="biased"
+                    )
+                add_bias(j, products[j], biaseds[j // PAIR])
 
             weight, j = unit_at(s - 1)
             if weight == "W1":
@@ -290,11 +326,17 @@ def tile_moelayer_k_kernel(tc, x, W1, b1, W2, b2, temperature, out):
             if weight == "W2":
                 if j % EXPERT_UNITS == 0:
                     ys[j // EXPERT_UNITS] = psum_y.tile([P, D], F32, name="y")
-                second_matmul(j, ys[j // EXPERT_UNITS], *h_operands[j], *quantise(groupeds[s - 1]))
+                parts = UNIT_PASSES if s == len(stream) else 1
+                second_matmul(
+                    j,
+                    ys[j // EXPERT_UNITS],
+                    *h_operands[j // PAIR],
+                    *quantise(groupeds[s - 1], parts),
+                )
 
             weight, j = unit_at(s - 3)
-            if weight == "W1":
-                hs[j] = relu(biaseds[j])
+            if weight == "W1" and j % PAIR == PAIR - 1:
+                hs[j // PAIR] = relu(biaseds[j // PAIR])
 
             weight, j = unit_at(s - 2)
             if weight == "W2" and j % EXPERT_UNITS == EXPERT_UNITS - 1:

import math
from contextlib import ExitStack

import concourse.mybir as mybir
from concourse.masks import make_identity

BF16 = mybir.dt.bfloat16
F32 = mybir.dt.float32
U32 = mybir.dt.uint32
U8 = mybir.dt.uint8
FP8X4 = mybir.dt.float8_e4m3fn_x4
ALU = mybir.AluOpType
ACT = mybir.ActivationFunctionType

P = 128
PACK = 4
K_PASS = P * PACK

E = 2
TOKENS = 128
D = 512
H = 8192
PASSES = H // K_PASS

UNIT = 1024
UNIT_PASSES = UNIT // D
EXPERT_UNITS = H // UNIT
N_UNITS = E * EXPERT_UNITS
LEAD = 4
PAIR = 2
LOAD_AHEAD = 7

VECTOR_COLUMNS = {"W1": 172, "W2": 140}
TENSOR_COLUMNS = 192
STAGE_AHEAD = 2
HEAD_PIECE = 256
HEAD_UNITS = 2
HEAD_VECTOR_COLUMNS = 160

B2_LOAD_STEP = N_UNITS // 2
B2_SCALE_STEP = B2_LOAD_STEP + 4

CLAMP_MAX = math.log(100.0)

FLOPS = 2 * (2 * E * TOKENS * D * H)


def tile_moelayer_k_kernel(tc, x, W1, b1, W2, b2, temperature, out):
    nc = tc.nc
    with ExitStack() as stack:
        stack.enter_context(nc.allow_non_contiguous_dma(reason="temperature: one element a partition"))
        stack.enter_context(tc.manual_schedule())
        const = stack.enter_context(tc.tile_pool(name="const", bufs=1))
        raw_pool = stack.enter_context(tc.tile_pool(name="raw", bufs=LOAD_AHEAD + 1))
        grouped_pool = stack.enter_context(tc.tile_pool(name="grouped", bufs=4))
        operand_pool = stack.enter_context(tc.tile_pool(name="operand", bufs=3))
        hidden_pool = stack.enter_context(tc.tile_pool(name="hidden", bufs=LEAD + 1))
        psum_staged = stack.enter_context(tc.psum_pool(name="psum_staged", bufs=2))
        psum_hidden = stack.enter_context(tc.psum_pool(name="psum_hidden", bufs=2 * UNIT_PASSES))
        psum_y = stack.enter_context(tc.psum_pool(name="psum_y", bufs=E))

        def load_unit(weight, j, piece=UNIT):
            e, i = j // EXPERT_UNITS, j % EXPERT_UNITS
            raw = raw_pool.tile([P, PACK, UNIT], BF16, name="raw")
            if weight == "W1":
                for first in range(0, UNIT, piece):
                    columns = W1[e, :, i * UNIT + first : i * UNIT + first + piece]
                    nc.sync.dma_start(
                        out=raw[:, :, first : first + piece],
                        in_=columns.rearrange("(p t) w -> p t w", t=PACK),
                    )
            else:
                for q in range(UNIT_PASSES):
                    g = i * UNIT_PASSES + q
                    rows = W2[e, g * K_PASS : (g + 1) * K_PASS, :]
                    nc.sync.dma_start(
                        out=raw[:, :, q * D : (q + 1) * D],
                        in_=rows.rearrange("(p t) d -> p t d", t=PACK),
                    )
            return raw

        def views(weight, grouped, raw, q, first, last):
            order = "p (q u m) t -> p q m t u" if weight == "W1" else "p (q m u) t -> p q m t u"
            fours = slice(first // PACK, last // PACK)
            to = grouped[:].rearrange(order, q=UNIT_PASSES, u=PACK)
            frm = raw[:].rearrange("p t (q m u) -> p q m t u", q=UNIT_PASSES, u=PACK)
            return to[:, q, fours, :, :], frm[:, q, fours, :, :]

        def regroup(weight, raw, staged):
            grouped = grouped_pool.tile([P, UNIT, PACK], BF16, name="grouped", align_bytes=64)
            both = slice(0, UNIT_PASSES)
            middle = VECTOR_COLUMNS[weight]
            to, frm = views(weight, grouped, raw, both, 0, middle)
            nc.vector.tensor_copy(out=to, in_=frm)
            if weight == "W1":
                to, frm = views(weight, grouped, raw, both, middle, D)
                nc.scalar.copy(out=to, in_=frm)
                return grouped
            for q, last in ((0, D), (1, D - TENSOR_COLUMNS)):
                to, frm = views(weight, grouped, raw, q, middle, last)
                nc.scalar.copy(out=to, in_=frm)
            nc.scalar.copy(out=grouped[:, UNIT - TENSOR_COLUMNS :, :], in_=staged[:])
            return grouped

        def stage(raw):
            first = UNIT - TENSOR_COLUMNS
            staged = psum_staged.tile([P, TENSOR_COLUMNS, PACK], BF16, name="staged")
            for w in range(0, TENSOR_COLUMNS, P):
                last = min(w + P, TENSOR_COLUMNS)
                nc.tensor.matmul(
                    out=staged[:, w:last, :],
                    lhsT=identity[:],
                    rhs=raw[:, :, first + w : first + last].rearrange("p t w -> p w t"),
                    start=True,
                    stop=True,
                )
            return staged

        def regroup_in_pieces(weight, raw, vector_columns):
            grouped = grouped_pool.tile([P, UNIT, PACK], BF16, name="grouped", align_bytes=64)
            for q in range(UNIT_PASSES):
                for first in range(0, D, HEAD_PIECE):
                    middle = first + vector_columns
                    to, frm = views(weight, grouped, raw, q, first, middle)
                    nc.vector.tensor_copy(out=to, in_=frm)
                    to, frm = views(weight, grouped, raw, q, middle, first + HEAD_PIECE)
                    nc.scalar.copy(out=to, in_=frm)
            return grouped

        def quantise(grouped, parts=1):
            words = operand_pool.tile([P, UNIT], U32, name="words", align_bytes=64)
            scales = operand_pool.tile([P, UNIT], U8, name="scales", align_bytes=64)
            for part in range(parts):
                span = slice(part * UNIT // parts, (part + 1) * UNIT // parts)
                nc.vector.quantize_mx(
                    out=words[:, span].bitcast(FP8X4),
                    scales=scales[:, span],
                    in_=grouped[:, span, :].rearrange("p w t -> p (w t)"),
                )
            return words, scales

        stream = [("W1", j) for j in range(LEAD)]
        for j in range(N_UNITS - LEAD):
            stream.extend([("W2", j), ("W1", j + LEAD)])
        stream.extend([("W2", j) for j in range(N_UNITS - LEAD, N_UNITS)])

        def unit_at(s):
            return stream[s] if 0 <= s < len(stream) else (None, None)

        warm = const.tile([P, 1], F32)
        nc.vector.memset(warm[:], 0.0)
        nc.scalar.activation(out=warm[:], in_=warm[:], func=ACT.Exp)

        b1_rows = const.tile([P, K_PASS], BF16)
        nc.vector.memset(b1_rows[:], 0.0)
        identity = const.tile([P, P], BF16)
        make_identity(nc, identity[:])

        raws = {}
        raws[0] = load_unit(*stream[0], piece=HEAD_PIECE)
        x_rows = const.tile([P, E, D], BF16)
        nc.sync.dma_start(out=x_rows[:], in_=x.rearrange("(e n) k -> n e k", e=E))
        nc.scalar.dma_start(
            out=b1_rows[0 : E * PASSES, :], in_=b1.rearrange("e (g c) -> (e g) c", c=K_PASS)
        )
        temp = const.tile([P, 1], BF16)
        nc.scalar.dma_start(out=temp[:], in_=temperature.partition_broadcast(P))
        for s in range(1, LOAD_AHEAD):
            raws[s] = load_unit(*stream[s], piece=HEAD_PIECE if s < HEAD_UNITS else UNIT)

        temp_clamped = const.tile([P, 1], F32)
        logit_scale = const.tile([P, 1], F32)

        def prepare_scale():
            nc.vector.tensor_scalar_min(out=temp_clamped[:], in0=temp[:], scalar1=CLAMP_MAX)
            nc.scalar.activation(out=logit_scale[:], in_=temp_clamped[:], func=ACT.Exp)

        x_words = const.tile([P, E * TOKENS], U32, align_bytes=64)
        x_scales = const.tile([P, E * TOKENS], U8, align_bytes=64)
        b1_t = const.tile([P, E * PASSES, PACK], F32)

        def prepare_x_and_b1():
            x_t = psum_staged.tile([P, E, PACK, TOKENS], BF16, name="staged")
            for e in range(E):
                for t in range(PACK):
                    nc.tensor.transpose(
                        x_t[:, e, t, :], x_rows[:, e, t : K_PASS : PACK], identity[:]
                    )
            x_grouped = const.tile([P, E, TOKENS, PACK], BF16, align_bytes=64)
            nc.vector.tensor_copy(out=x_grouped[:], in_=x_t[:].rearrange("p e t n -> p e n t"))
            b1_t_psum = psum_staged.tile([P, PACK, P], BF16, name="staged")
            for t in range(PACK):
                nc.tensor.transpose(
                    b1_t_psum[:, t, :], b1_rows[:, t : K_PASS : PACK], identity[:]
                )
            nc.vector.tensor_copy(
                out=b1_t[:], in_=b1_t_psum[:, :, 0 : E * PASSES].rearrange("p t r -> p r t")
            )
            nc.vector.quantize_mx(
                out=x_words[:].bitcast(FP8X4),
                scales=x_scales[:],
                in_=x_grouped[:].rearrange("p e n t -> p (e n t)"),
            )

        b2_all = const.tile([P, E * D], BF16)
        b2_scaled = const.tile([P, E * D], F32)

        def first_matmul(j, w1_words, w1_scales):
            tokens = slice((j // EXPERT_UNITS) * TOKENS, (j // EXPERT_UNITS + 1) * TOKENS)
            product = []
            for q in range(UNIT_PASSES):
                bank = psum_hidden.tile([P, PACK, TOKENS], F32, name="bank")
                for t in range(PACK):
                    columns = slice((q * PACK + t) * P, (q * PACK + t + 1) * P)
                    nc.tensor.matmul_mx(
                        out=bank[:, t, :],
                        lhsT=w1_words[:, columns].bitcast(FP8X4),
                        lhsT_scale=w1_scales[:, columns],
                        rhs=x_words[:, tokens].bitcast(FP8X4),
                        rhs_scale=x_scales[:, tokens],
                        start=True,
                        stop=True,
                    )
                product.append(bank)
            return product

        def add_bias(j, product, biased):
            for q in range(UNIT_PASSES):
                nc.vector.tensor_tensor(
                    out=biased[:, j % PAIR, q, :, :],
                    in0=product[q][:].rearrange("p t n -> p n t"),
                    in1=b1_t[:, j * UNIT_PASSES + q : j * UNIT_PASSES + q + 1, :].to_broadcast([P, TOKENS, PACK]),
                    op=ALU.add,
                )

        def relu(biased):
            h = hidden_pool.tile([P, PAIR * UNIT_PASSES * TOKENS * PACK], BF16, name="h", align_bytes=64)
            nc.vector.tensor_scalar_max(
                out=h[:], in0=biased[:].rearrange("p j q n t -> p (j q n t)"), scalar1=0.0
            )
            return h

        def quantise_hidden(h):
            h_words = hidden_pool.tile([P, PAIR * UNIT_PASSES * TOKENS], U32, name="h_words", align_bytes=64)
            h_scales = hidden_pool.tile([P, PAIR * UNIT_PASSES * TOKENS], U8, name="h_scales", align_bytes=64)
            nc.vector.quantize_mx(out=h_words[:].bitcast(FP8X4), scales=h_scales[:], in_=h[:])
            return h_words, h_scales

        def second_matmul(j, y, h_words, h_scales, w2_words, w2_scales):
            for q in range(UNIT_PASSES):
                g = (j % EXPERT_UNITS) * UNIT_PASSES + q
                first = ((j % PAIR) * UNIT_PASSES + q) * TOKENS
                nc.tensor.matmul_mx(
                    out=y[:],
                    lhsT=h_words[:, first : first + TOKENS].bitcast(FP8X4),
                    lhsT_scale=h_scales[:, first : first + TOKENS],
                    rhs=w2_words[:, q * D : (q + 1) * D].bitcast(FP8X4),
                    rhs_scale=w2_scales[:, q * D : (q + 1) * D],
                    start=(g == 0),
                    stop=(g == PASSES - 1),
                )

        def finish(e, y):
            result = hidden_pool.tile([P, D], F32, name="result")
            for half in (slice(0, D // 2), slice(D // 2, D)):
                nc.vector.scalar_tensor_tensor(
                    out=result[:, half],
                    in0=y[:, half],
                    scalar=logit_scale[:, 0:1],
                    in1=b2_scaled[:, e * D + half.start : e * D + half.stop],
                    op0=ALU.mult,
                    op1=ALU.add,
                )
                nc.sync.dma_start(
                    out=out[e * TOKENS : (e + 1) * TOKENS, half], in_=result[:, half]
                )

        stageds = {}
        groupeds = {}
        products = {}
        biaseds = {}
        hs = {}
        h_operands = {}
        ys = {}
        for s in range(len(stream) + 2):
            if s + LOAD_AHEAD < len(stream):
                raws[s + LOAD_AHEAD] = load_unit(*stream[s + LOAD_AHEAD])
            weight, j = unit_at(s + STAGE_AHEAD)
            if weight == "W2":
                stageds[s + STAGE_AHEAD] = stage(raws[s + STAGE_AHEAD])
            if s < len(stream):
                if s == 0:
                    groupeds[s] = regroup_in_pieces(stream[s][0], raws[s], HEAD_VECTOR_COLUMNS)
                elif s < HEAD_UNITS:
                    groupeds[s] = regroup_in_pieces(stream[s][0], raws[s], HEAD_PIECE // 2)
                else:
                    groupeds[s] = regroup(stream[s][0], raws[s], stageds.get(s))
            if s == 0:
                prepare_x_and_b1()
            if s == 4:
                prepare_scale()
            if s == B2_LOAD_STEP:
                nc.sync.dma_start(
                    out=b2_all[:], in_=b2.rearrange("e d -> (e d)").partition_broadcast(P)
                )
            if s == B2_SCALE_STEP:
                nc.vector.tensor_scalar_mul(
                    out=b2_scaled[:], in0=b2_all[:], scalar1=logit_scale[:, 0:1]
                )

            weight, j = unit_at(s - 4)
            if weight == "W1" and j % PAIR == PAIR - 1:
                h_operands[j // PAIR] = quantise_hidden(hs[j // PAIR])

            weight, j = unit_at(s - 3)
            if weight == "W1":
                if j % PAIR == 0:
                    biaseds[j // PAIR] = hidden_pool.tile(
                        [P, PAIR, UNIT_PASSES, TOKENS, PACK], BF16, name="biased"
                    )
                add_bias(j, products[j], biaseds[j // PAIR])

            weight, j = unit_at(s - 1)
            if weight == "W1":
                products[j] = first_matmul(j, *quantise(groupeds[s - 1]))
            if weight == "W2":
                if j % EXPERT_UNITS == 0:
                    ys[j // EXPERT_UNITS] = psum_y.tile([P, D], F32, name="y")
                parts = UNIT_PASSES if s == len(stream) else 1
                second_matmul(
                    j,
                    ys[j // EXPERT_UNITS],
                    *h_operands[j // PAIR],
                    *quantise(groupeds[s - 1], parts),
                )

            weight, j = unit_at(s - 3)
            if weight == "W1" and j % PAIR == PAIR - 1:
                hs[j // PAIR] = relu(biaseds[j // PAIR])

            weight, j = unit_at(s - 2)
            if weight == "W2" and j % EXPERT_UNITS == EXPERT_UNITS - 1:
                finish(j // EXPERT_UNITS, ys[j // EXPERT_UNITS])
